import numpy as np
import ml_dtypes


def mxq(x, axis, fmt="e4m3"):
    dtype, down = {"e4m3": (ml_dtypes.float8_e4m3fn, 7), "e5m2": (ml_dtypes.float8_e5m2, 14)}[fmt]
    v = np.moveaxis(np.asarray(x, np.float32).astype(ml_dtypes.bfloat16).astype(np.float64), axis, -1)
    blocks = v.reshape(v.shape[:-1] + (-1, 32))
    amax = np.abs(blocks).max(-1, keepdims=True)
    byte = np.maximum(np.where(amax > 0, np.frexp(amax)[1] - 1 + 127, 0) - down, 1)
    scale = np.exp2(byte - 127.0)
    codes = (blocks / scale).astype(np.float32).astype(dtype).astype(np.float64)
    return np.moveaxis((codes * scale).reshape(v.shape), -1, axis)


WIDE = False


def mx_kscale(k):
    if not WIDE:
        return np.ones(k)
    levels = np.array([10, -10, 5, -5, 0])
    a = np.random.permutation(np.resize(levels, k // 512 * 4)).reshape(k // 512, 4)
    idx = np.arange(k)
    return np.exp2(a[idx // 512, idx % 128 // 32])


BF16 = ml_dtypes.bfloat16


def bf(x):
    return np.asarray(x, np.float32).astype(BF16)


def f64(x):
    return np.asarray(x).astype(np.float64)


E2M1 = np.array([0.0, 0.5, 1.0, 1.5, 2.0, 3.0, 4.0, 6.0, -0.0, -0.5, -1.0, -1.5, -2.0, -3.0, -4.0, -6.0])


def pack_weight(w, fmt):
    k, n = w.shape
    w = f64(bf(w)).reshape(k // 32, 32, n)
    amax = np.abs(w).max(1)
    if fmt == "e4m3":
        byte = np.frexp(amax)[1] - 1 + 127 - 7
    else:
        mant, ex = np.frexp(amax / 6.0)
        byte = np.where(mant > 0.5, ex, ex - 1) + 127
    byte = np.clip(np.where(amax > 0, byte, 1), 1, 254)
    scaled = (w * np.exp2(127.0 - byte)[:, None, :]).reshape(k, n).astype(np.float32)
    by_word = np.ascontiguousarray(scaled.reshape(k // 512, 128, 4, n).transpose(0, 1, 3, 2))
    if fmt == "e4m3":
        words = by_word.astype(ml_dtypes.float8_e4m3fn).view(np.uint8)
    else:
        c = by_word.astype(ml_dtypes.float4_e2m1fn).view(np.uint8) & 0xF
        words = c[..., 0::2] | (c[..., 1::2] << 4)
    return np.ascontiguousarray(words), np.ascontiguousarray(byte.astype(np.uint8).reshape(k // 512, 16, n))


def unpack_weight(words, scales, fmt):
    g, p, n, _ = words.shape
    if fmt == "e4m3":
        vals = np.ascontiguousarray(words).view(ml_dtypes.float8_e4m3fn).astype(np.float64)
    else:
        nib = np.empty((g, p, n, 4), np.uint8)
        nib[..., 0::2] = words & 0xF
        nib[..., 1::2] = words >> 4
        vals = E2M1[nib]
    vals = vals * np.repeat(np.exp2(scales.astype(np.float64) - 127.0), 8, axis=1)[..., None]
    return vals.transpose(0, 1, 3, 2).reshape(g * 512, n)

def pack4(w):
    words, scales = pack_weight(w, "e2m1")
    return words.reshape(words.shape[0], 128, -1), scales


def unpack4(words, scales):
    return unpack_weight(words.reshape(words.shape[0], 128, -1, 2), scales, "e2m1")


B, P, D = 4096, 2, 512
IN = P * D


def sigmoid(v):
    return 1.0 / (1.0 + np.exp(-v))


def setup_inputs():
    s = mx_kscale(D)
    sf = np.tile(s, P)
    x = bf(np.random.standard_normal((B, IN)) * sf)
    stack = np.random.standard_normal((P, D, D)) / np.sqrt(D) / s[None, :, None] * s[None, None, :]
    words, scales = pack4(stack.reshape(-1, D))
    return {"x": x,
            "weights_words": words,
            "weights_scales": scales,
            "bias": bf(np.random.standard_normal(IN) * 0.3 * sf),
            "gain": bf(1.3 + 0.1 * np.random.standard_normal(1)),
            "norm_bias": bf((0.3 + 0.05 * np.random.standard_normal(1)) * s.min()),
            "gamma": bf(0.5 + 0.3 * np.random.standard_normal(IN)),
            "beta": bf(np.random.standard_normal(IN) / sf)}


def reference(x, weights_words, weights_scales, bias, gain, norm_bias, gamma, beta):
    x, gamma = f64(x), f64(gamma)
    x_norm = x * f64(gain) + f64(norm_bias)
    xp = x_norm.reshape(B, P, D)
    yp = mxq(xp, 2, "e4m3").transpose(1, 0, 2) @ unpack4(weights_words, weights_scales).reshape(P, D, D)
    y = yp.transpose(1, 0, 2).reshape(B, IN) + f64(bias)
    mult = gamma + sigmoid(f64(beta) * y) * (1.0 - gamma)
    o = mult * y
    return o + x

@@ -1,0 +1,265 @@
+from contextlib import ExitStack
+
+import concourse.mybir as mybir
+from concourse.masks import make_identity
+
+F32 = mybir.dt.float32
+BF16 = mybir.dt.bfloat16
+I32 = mybir.dt.int32
+U32 = mybir.dt.uint32
+U8 = mybir.dt.uint8
+FP8X4 = mybir.dt.float8_e4m3fn_x4
+FP4X4 = mybir.dt.float4_e2m1fn_x4
+ALU = mybir.AluOpType
+ACT = mybir.ActivationFunctionType
+
+P = 128
+PACK = 4
+ROWS = 4096
+PARTS = 2
+PART = 512
+FEATURES = PARTS * PART
+
+ROUND = 512
+ROW_TILES = ROUND // P
+ROUNDS = ROWS // ROUND
+GROUPS = ROUNDS * PARTS
+F_TILES = PART // P
+PAIR = 2
+STEPS = GROUPS * F_TILES // PAIR
+STEPS_PER_GROUP = F_TILES // PAIR
+HALF = ROUND // 2
+N_COLS = FEATURES // P
+XT_BANKS = 2
+LEAD = 4
+
+FLOPS = 2 * ROWS * FEATURES * PART
+
+
+def tile_better_transformer_t_e_kernel(
+    tc, x, weights_words, weights_scales, bias, gain, norm_bias, gamma, beta, out
+):
+    nc = tc.nc
+    with ExitStack() as ctx:
+        ctx.enter_context(tc.manual_schedule())
+        const = ctx.enter_context(tc.tile_pool(name="const", bufs=1))
+        x_pool = ctx.enter_context(tc.tile_pool(name="x_pool", bufs=ROUNDS))
+        grouped_pool = ctx.enter_context(tc.tile_pool(name="grouped_pool", bufs=2))
+        codes_pool = ctx.enter_context(tc.tile_pool(name="codes_pool", bufs=3))
+        gate_pool = ctx.enter_context(tc.tile_pool(name="gate_pool", bufs=3 * PAIR))
+        act_pool = ctx.enter_context(tc.tile_pool(name="act_pool", bufs=2 * PAIR))
+        out_pool = ctx.enter_context(tc.tile_pool(name="out_pool", bufs=3))
+        xt_psum = ctx.enter_context(tc.psum_pool(name="xt_psum", bufs=XT_BANKS))
+        y_psum = ctx.enter_context(tc.psum_pool(name="y_psum", bufs=2 * PAIR))
+        back_psum = ctx.enter_context(tc.psum_pool(name="back_psum", bufs=PAIR))
+
+        x_rounds = x.rearrange("(r p t) f -> r p t f", p=P, t=ROW_TILES)
+        out_rounds = out.rearrange("(r p t) f -> r p t f", p=P, t=ROW_TILES)
+
+        def load_round(r):
+            x_sb = x_pool.tile([P, ROW_TILES, FEATURES], BF16)
+            for h in range(2):
+                tiles = slice(2 * h, 2 * h + 2)
+                nc.sync.dma_start(out=x_sb[:, tiles, :], in_=x_rounds[r, :, tiles, :])
+            return x_sb
+
+        x_tiles = [load_round(0)]
+
+        gain_bf = const.tile([P, 1], BF16)
+        nc.scalar.dma_start(out=gain_bf[:], in_=gain.partition_broadcast(P))
+        norm_bias_bf = const.tile([P, 1], BF16)
+        nc.scalar.dma_start(out=norm_bias_bf[:], in_=norm_bias.partition_broadcast(P))
+
+        w_words = const.tile([P, PARTS, 2 * PART], U8, align_bytes=64)
+        nc.sync.dma_start(
+            out=w_words[:].bitcast(I32),
+            in_=weights_words.rearrange("g p n -> p g n").bitcast(I32),
+        )
+        w_scales = const.tile([P, PARTS, PART], U8, align_bytes=64)
+        nc.vector.memset(w_scales[:].bitcast(I32), 0)
+        for quadrant in range(4):
+            nc.sync.dma_start(
+                out=w_scales[32 * quadrant : 32 * quadrant + 4].bitcast(I32),
+                in_=weights_scales[:, 4 * quadrant : 4 * quadrant + 4, :]
+                .rearrange("g q n -> q g n")
+                .bitcast(I32),
+            )
+
+        for r in range(1, ROUNDS):
+            x_tiles.append(load_round(r))
+
+        rows_bf = const.tile([P, P], BF16)
+        nc.vector.memset(rows_bf[:], 0.0)
+        for i, vector in enumerate((bias, beta, gamma)):
+            nc.gpsimd.dma_start(
+                out=rows_bf[i * N_COLS : (i + 1) * N_COLS, :],
+                in_=vector.rearrange("(j p) -> j p", p=P),
+            )
+
+        ident = const.tile([P, P], F32)
+        make_identity(nc, ident[:])
+
+        warm = const.tile([P, 1], F32)
+        nc.vector.memset(warm[:], 0.0)
+        nc.scalar.activation(out=warm[:], in_=warm[:], func=ACT.Sigmoid)
+
+        gain_col = const.tile([P, 1], F32)
+        nc.vector.tensor_copy(out=gain_col[:], in_=gain_bf[:])
+        norm_bias_col = const.tile([P, 1], F32)
+        nc.vector.tensor_copy(out=norm_bias_col[:], in_=norm_bias_bf[:])
+
+        cols = const.tile([P, 3 * N_COLS], F32)
+        bias_cols = cols[:, 0:N_COLS]
+        beta_cols = cols[:, N_COLS : 2 * N_COLS]
+        gamma_cols = cols[:, 2 * N_COLS : 3 * N_COLS]
+        beta_bias_cols = const.tile([P, N_COLS], F32)
+        one_minus_gamma_cols = const.tile([P, N_COLS], F32)
+
+        def make_tables():
+            rows_f32 = const.tile([P, P], F32)
+            nc.vector.tensor_copy(out=rows_f32[:], in_=rows_bf[:])
+            cols_ps = back_psum.tile([P, ROW_TILES, P], F32, name="back_ps")
+            nc.tensor.transpose(cols_ps[:, 0, :], rows_f32[:], ident[:])
+            nc.vector.tensor_copy(out=cols[:], in_=cols_ps[:, 0, 0 : 3 * N_COLS])
+            nc.vector.tensor_mul(out=beta_bias_cols[:], in0=beta_cols, in1=bias_cols)
+            nc.vector.tensor_scalar(
+                out=one_minus_gamma_cols[:],
+                in0=gamma_cols,
+                scalar1=-1.0,
+                scalar2=1.0,
+                op0=ALU.mult,
+                op1=ALU.add,
+            )
+
+        grouped_tiles = {}
+        operands = {}
+        products = {}
+        out_tiles = {}
+
+        def transpose_half(bank):
+            group, h = divmod(bank, 2)
+            r, g = divmod(group, PARTS)
+            if h == 0:
+                grouped = grouped_pool.tile([P, ROUND, PACK], BF16, align_bytes=64)
+                grouped_tiles[group] = grouped
+            x_words = x_tiles[r][:].bitcast(F32)
+            first_word = g * PART // 2
+            xt_ps = xt_psum.tile([P, 2, HALF], F32)
+            for i in range(2):
+                for u in range(2):
+                    nc.tensor.transpose(
+                        xt_ps[:, u, i * P : (i + 1) * P],
+                        x_words[:, 2 * h + i, first_word + u : first_word + PART // 2 : 2],
+                        ident[:],
+                    )
+            nc.scalar.activation(
+                out=grouped_tiles[group][:, h * HALF : (h + 1) * HALF, :].rearrange(
+                    "p c (u e) -> p c u e", e=2
+                ),
+                in_=xt_ps[:].bitcast(BF16).rearrange("p u (c e) -> p c u e", e=2),
+                func=ACT.Identity,
+                scale=gain_col[:, 0:1],
+                bias=norm_bias_col[:, 0:1],
+            )
+
+        def quantise(group):
+            codes = codes_pool.tile([P, ROUND], U32, align_bytes=64)
+            scales = codes_pool.tile([P, ROUND], U8, align_bytes=64)
+            nc.vector.quantize_mx(
+                out=codes[:].bitcast(FP8X4),
+                scales=scales[:],
+                in_=grouped_tiles[group][:].rearrange("p c j -> p (c j)"),
+            )
+            operands[group] = (codes, scales)
+
+        def multiply_and_gate(step):
+            group = step // STEPS_PER_GROUP
+            g = group % PARTS
+            codes, scales = operands[group]
+            for i in range(PAIR):
+                m = (step % STEPS_PER_GROUP) * PAIR + i
+                j = g * F_TILES + m
+                y_ps = y_psum.tile([P, ROUND], F32)
+                nc.tensor.matmul_mx(
+                    out=y_ps[:],
+                    lhsT=w_words[:, g, 2 * m * P : 2 * (m + 1) * P].bitcast(FP4X4),
+                    lhsT_scale=w_scales[:, g, m * P : (m + 1) * P],
+                    rhs=codes[:].bitcast(FP8X4),
+                    rhs_scale=scales[:],
+                    start=True,
+                    stop=True,
+                )
+                gate = gate_pool.tile([P, ROUND], F32)
+                nc.scalar.activation(
+                    out=gate[:],
+                    in_=y_ps[:],
+                    func=ACT.Sigmoid,
+                    scale=beta_cols[:, j : j + 1],
+                    bias=beta_bias_cols[:, j : j + 1],
+                )
+                nc.gpsimd.tensor_scalar(
+                    out=gate[:],
+                    in0=gate[:],
+                    scalar1=one_minus_gamma_cols[:, j : j + 1],
+                    scalar2=gamma_cols[:, j : j + 1],
+                    op0=ALU.mult,
+                    op1=ALU.add,
+                )
+                products[(step, i)] = (y_ps, gate)
+
+        def activate_and_store(step):
+            group = step // STEPS_PER_GROUP
+            r, g = divmod(group, PARTS)
+            if step % STEPS_PER_GROUP == 0:
+                out_sb = out_pool.tile([P, ROW_TILES, PART], F32)
+                out_tiles[group] = out_sb
+            acts = []
+            for i in range(PAIR):
+                m = (step % STEPS_PER_GROUP) * PAIR + i
+                j = g * F_TILES + m
+                y_ps, gate = products[(step, i)]
+                act = act_pool.tile([P, ROUND], F32)
+                nc.vector.scalar_tensor_tensor(
+                    out=act[:],
+                    in0=y_ps[:],
+                    scalar=bias_cols[:, j : j + 1],
+                    in1=gate[:],
+                    op0=ALU.add,
+                    op1=ALU.mult,
+                )
+                acts.append(act)
+            backs = []
+            for i in range(PAIR):
+                back_ps = back_psum.tile([P, ROW_TILES, P], F32)
+                for t in range(ROW_TILES):
+                    nc.tensor.transpose(back_ps[:, t, :], acts[i][:, t * P : (t + 1) * P], ident[:])
+                backs.append(back_ps)
+            for i in range(PAIR):
+                m = (step % STEPS_PER_GROUP) * PAIR + i
+                nc.vector.tensor_tensor(
+                    out=out_tiles[group][:, :, m * P : (m + 1) * P],
+                    in0=backs[i][:],
+                    in1=x_tiles[r][:, :, g * PART + m * P : g * PART + (m + 1) * P],
+                    op=ALU.add,
+                )
+            if step % STEPS_PER_GROUP == STEPS_PER_GROUP - 1:
+                nc.sync.dma_start(
+                    out=out_rounds[r, :, :, g * PART : (g + 1) * PART],
+                    in_=out_tiles[group][:],
+                )
+
+        for bank in range(XT_BANKS):
+            transpose_half(bank)
+        make_tables()
+        for bank in range(XT_BANKS, LEAD):
+            transpose_half(bank)
+        quantise(0)
+        multiply_and_gate(0)
+        for step in range(STEPS):
+            if step % STEPS_PER_GROUP == 0 and step // STEPS_PER_GROUP + 1 < GROUPS:
+                quantise(step // STEPS_PER_GROUP + 1)
+            if step + 1 < STEPS:
+                multiply_and_gate(step + 1)
+            activate_and_store(step)
+            if step + LEAD < STEPS:
+                transpose_half(step + LEAD)

@@ -31,7 +31,9 @@ STEPS_PER_GROUP = F_TILES // PAIR
 HALF = ROUND // 2
 N_COLS = FEATURES // P
 XT_BANKS = 2
-LEAD = 4
+TRANSPOSE_LEAD = 5
+NORMALISE_LEAD = 4
+QUANTISE_LEAD = 2
 
 FLOPS = 2 * ROWS * FEATURES * PART
 
@@ -91,7 +93,7 @@ def tile_better_transformer_t_e_kernel(
         rows_bf = const.tile([P, P], BF16)
         nc.vector.memset(rows_bf[:], 0.0)
         for i, vector in enumerate((bias, beta, gamma)):
-            nc.gpsimd.dma_start(
+            nc.scalar.dma_start(
                 out=rows_bf[i * N_COLS : (i + 1) * N_COLS, :],
                 in_=vector.rearrange("(j p) -> j p", p=P),
             )
@@ -131,17 +133,15 @@ def tile_better_transformer_t_e_kernel(
                 op1=ALU.add,
             )
 
+        transposed = {}
         grouped_tiles = {}
         operands = {}
         products = {}
         out_tiles = {}
 
-        def transpose_half(bank):
-            group, h = divmod(bank, 2)
+        def transpose_half(half):
+            group, h = divmod(half, 2)
             r, g = divmod(group, PARTS)
-            if h == 0:
-                grouped = grouped_pool.tile([P, ROUND, PACK], BF16, align_bytes=64)
-                grouped_tiles[group] = grouped
             x_words = x_tiles[r][:].bitcast(F32)
             first_word = g * PART // 2
             xt_ps = xt_psum.tile([P, 2, HALF], F32)
@@ -152,6 +152,14 @@ def tile_better_transformer_t_e_kernel(
                         x_words[:, 2 * h + i, first_word + u : first_word + PART // 2 : 2],
                         ident[:],
                     )
+            transposed[half] = xt_ps
+
+        def normalise_half(half):
+            group, h = divmod(half, 2)
+            if h == 0:
+                grouped = grouped_pool.tile([P, ROUND, PACK], BF16, align_bytes=64)
+                grouped_tiles[group] = grouped
+            xt_ps = transposed[half]
             nc.scalar.activation(
                 out=grouped_tiles[group][:, h * HALF : (h + 1) * HALF, :].rearrange(
                     "p c (u e) -> p c u e", e=2
@@ -248,18 +256,21 @@ def tile_better_transformer_t_e_kernel(
                     in_=out_tiles[group][:],
                 )
 
-        for bank in range(XT_BANKS):
-            transpose_half(bank)
-        make_tables()
-        for bank in range(XT_BANKS, LEAD):
-            transpose_half(bank)
-        quantise(0)
-        multiply_and_gate(0)
-        for step in range(STEPS):
-            if step % STEPS_PER_GROUP == 0 and step // STEPS_PER_GROUP + 1 < GROUPS:
-                quantise(step // STEPS_PER_GROUP + 1)
-            if step + 1 < STEPS:
+        def run_step(step):
+            group, first = divmod(step + QUANTISE_LEAD, STEPS_PER_GROUP)
+            if first == 0 and 0 <= group < GROUPS:
+                quantise(group)
+            if 0 <= step + 1 < STEPS:
                 multiply_and_gate(step + 1)
-            activate_and_store(step)
-            if step + LEAD < STEPS:
-                transpose_half(step + LEAD)
+            if 0 <= step:
+                activate_and_store(step)
+            if 0 <= step + NORMALISE_LEAD < STEPS:
+                normalise_half(step + NORMALISE_LEAD)
+            if step + TRANSPOSE_LEAD < STEPS:
+                transpose_half(step + TRANSPOSE_LEAD)
+
+        for step in range(-TRANSPOSE_LEAD, XT_BANKS - TRANSPOSE_LEAD):
+            run_step(step)
+        make_tables()
+        for step in range(XT_BANKS - TRANSPOSE_LEAD, STEPS):
+            run_step(step)

@@ -26,14 +26,15 @@ ROUNDS = ROWS // ROUND
 GROUPS = ROUNDS * PARTS
 F_TILES = PART // P
 PAIR = 2
-STEPS = GROUPS * F_TILES // PAIR
+TILES = GROUPS * F_TILES
+STEPS = TILES // PAIR
 STEPS_PER_GROUP = F_TILES // PAIR
 HALF = ROUND // 2
 N_COLS = FEATURES // P
 XT_BANKS = 2
-TRANSPOSE_LEAD = 5
-NORMALISE_LEAD = 4
-QUANTISE_LEAD = 2
+Y_BANKS = 4
+INPUT_LEAD = 6
+QUANTISE_LEAD = 3
 
 FLOPS = 2 * ROWS * FEATURES * PART
 
@@ -48,11 +49,11 @@ def tile_better_transformer_t_e_kernel(
         x_pool = ctx.enter_context(tc.tile_pool(name="x_pool", bufs=ROUNDS))
         grouped_pool = ctx.enter_context(tc.tile_pool(name="grouped_pool", bufs=2))
         codes_pool = ctx.enter_context(tc.tile_pool(name="codes_pool", bufs=3))
-        gate_pool = ctx.enter_context(tc.tile_pool(name="gate_pool", bufs=3 * PAIR))
+        gate_pool = ctx.enter_context(tc.tile_pool(name="gate_pool", bufs=Y_BANKS + 2))
         act_pool = ctx.enter_context(tc.tile_pool(name="act_pool", bufs=2 * PAIR))
-        out_pool = ctx.enter_context(tc.tile_pool(name="out_pool", bufs=3))
+        out_pool = ctx.enter_context(tc.tile_pool(name="out_pool", bufs=4))
         xt_psum = ctx.enter_context(tc.psum_pool(name="xt_psum", bufs=XT_BANKS))
-        y_psum = ctx.enter_context(tc.psum_pool(name="y_psum", bufs=2 * PAIR))
+        y_psum = ctx.enter_context(tc.psum_pool(name="y_psum", bufs=Y_BANKS))
         back_psum = ctx.enter_context(tc.psum_pool(name="back_psum", bufs=PAIR))
 
         x_rounds = x.rearrange("(r p t) f -> r p t f", p=P, t=ROW_TILES)
@@ -137,6 +138,8 @@ def tile_better_transformer_t_e_kernel(
         grouped_tiles = {}
         operands = {}
         products = {}
+        acts = {}
+        backs = {}
         out_tiles = {}
 
         def transpose_half(half):
@@ -180,97 +183,101 @@ def tile_better_transformer_t_e_kernel(
             )
             operands[group] = (codes, scales)
 
-        def multiply_and_gate(step):
-            group = step // STEPS_PER_GROUP
+        def multiply_and_gate(j):
+            group, m = divmod(j, F_TILES)
             g = group % PARTS
+            col = g * F_TILES + m
             codes, scales = operands[group]
-            for i in range(PAIR):
-                m = (step % STEPS_PER_GROUP) * PAIR + i
-                j = g * F_TILES + m
-                y_ps = y_psum.tile([P, ROUND], F32)
-                nc.tensor.matmul_mx(
-                    out=y_ps[:],
-                    lhsT=w_words[:, g, 2 * m * P : 2 * (m + 1) * P].bitcast(FP4X4),
-                    lhsT_scale=w_scales[:, g, m * P : (m + 1) * P],
-                    rhs=codes[:].bitcast(FP8X4),
-                    rhs_scale=scales[:],
-                    start=True,
-                    stop=True,
-                )
-                gate = gate_pool.tile([P, ROUND], F32)
-                nc.scalar.activation(
-                    out=gate[:],
-                    in_=y_ps[:],
-                    func=ACT.Sigmoid,
-                    scale=beta_cols[:, j : j + 1],
-                    bias=beta_bias_cols[:, j : j + 1],
-                )
-                nc.gpsimd.tensor_scalar(
-                    out=gate[:],
-                    in0=gate[:],
-                    scalar1=one_minus_gamma_cols[:, j : j + 1],
-                    scalar2=gamma_cols[:, j : j + 1],
-                    op0=ALU.mult,
-                    op1=ALU.add,
-                )
-                products[(step, i)] = (y_ps, gate)
+            y_ps = y_psum.tile([P, ROUND], F32)
+            nc.tensor.matmul_mx(
+                out=y_ps[:],
+                lhsT=w_words[:, g, 2 * m * P : 2 * (m + 1) * P].bitcast(FP4X4),
+                lhsT_scale=w_scales[:, g, m * P : (m + 1) * P],
+                rhs=codes[:].bitcast(FP8X4),
+                rhs_scale=scales[:],
+                start=True,
+                stop=True,
+            )
+            gate = gate_pool.tile([P, ROUND], F32)
+            nc.scalar.activation(
+                out=gate[:],
+                in_=y_ps[:],
+                func=ACT.Sigmoid,
+                scale=beta_cols[:, col : col + 1],
+                bias=beta_bias_cols[:, col : col + 1],
+            )
+            nc.gpsimd.tensor_scalar(
+                out=gate[:],
+                in0=gate[:],
+                scalar1=one_minus_gamma_cols[:, col : col + 1],
+                scalar2=gamma_cols[:, col : col + 1],
+                op0=ALU.mult,
+                op1=ALU.add,
+            )
+            products[j] = (y_ps, gate)
 
-        def activate_and_store(step):
-            group = step // STEPS_PER_GROUP
+        def activate(j):
+            group, m = divmod(j, F_TILES)
+            col = (group % PARTS) * F_TILES + m
+            y_ps, gate = products[j]
+            act = act_pool.tile([P, ROUND], F32)
+            nc.vector.scalar_tensor_tensor(
+                out=act[:],
+                in0=y_ps[:],
+                scalar=bias_cols[:, col : col + 1],
+                in1=gate[:],
+                op0=ALU.add,
+                op1=ALU.mult,
+            )
+            acts[j] = act
+
+        def transpose_back(j):
+            back_ps = back_psum.tile([P, ROW_TILES, P], F32)
+            for t in range(ROW_TILES):
+                nc.tensor.transpose(back_ps[:, t, :], acts[j][:, t * P : (t + 1) * P], ident[:])
+            backs[j] = back_ps
+
+        def add_residual(j):
+            step, i = divmod(j, PAIR)
+            group, m = divmod(j, F_TILES)
             r, g = divmod(group, PARTS)
-            if step % STEPS_PER_GROUP == 0:
-                out_sb = out_pool.tile([P, ROW_TILES, PART], F32)
-                out_tiles[group] = out_sb
-            acts = []
-            for i in range(PAIR):
-                m = (step % STEPS_PER_GROUP) * PAIR + i
-                j = g * F_TILES + m
-                y_ps, gate = products[(step, i)]
-                act = act_pool.tile([P, ROUND], F32)
-                nc.vector.scalar_tensor_tensor(
-                    out=act[:],
-                    in0=y_ps[:],
-                    scalar=bias_cols[:, j : j + 1],
-                    in1=gate[:],
-                    op0=ALU.add,
-                    op1=ALU.mult,
-                )
-                acts.append(act)
-            backs = []
-            for i in range(PAIR):
-                back_ps = back_psum.tile([P, ROW_TILES, P], F32)
-                for t in range(ROW_TILES):
-                    nc.tensor.transpose(back_ps[:, t, :], acts[i][:, t * P : (t + 1) * P], ident[:])
-                backs.append(back_ps)
-            for i in range(PAIR):
-                m = (step % STEPS_PER_GROUP) * PAIR + i
-                nc.vector.tensor_tensor(
-                    out=out_tiles[group][:, :, m * P : (m + 1) * P],
-                    in0=backs[i][:],
-                    in1=x_tiles[r][:, :, g * PART + m * P : g * PART + (m + 1) * P],
-                    op=ALU.add,
-                )
-            if step % STEPS_PER_GROUP == STEPS_PER_GROUP - 1:
+            if i == 0:
+                out_sb = out_pool.tile([P, ROW_TILES, PAIR * P], F32)
+                out_tiles[step] = out_sb
+            first = g * PART + m * P
+            nc.vector.tensor_tensor(
+                out=out_tiles[step][:, :, i * P : (i + 1) * P],
+                in0=backs[j][:],
+                in1=x_tiles[r][:, :, first : first + P],
+                op=ALU.add,
+            )
+            if i == PAIR - 1:
                 nc.sync.dma_start(
-                    out=out_rounds[r, :, :, g * PART : (g + 1) * PART],
-                    in_=out_tiles[group][:],
+                    out=out_rounds[r, :, :, first + P - PAIR * P : first + P],
+                    in_=out_tiles[step][:],
                 )
 
         def run_step(step):
-            group, first = divmod(step + QUANTISE_LEAD, STEPS_PER_GROUP)
-            if first == 0 and 0 <= group < GROUPS:
-                quantise(group)
-            if 0 <= step + 1 < STEPS:
-                multiply_and_gate(step + 1)
-            if 0 <= step:
-                activate_and_store(step)
-            if 0 <= step + NORMALISE_LEAD < STEPS:
-                normalise_half(step + NORMALISE_LEAD)
-            if step + TRANSPOSE_LEAD < STEPS:
-                transpose_half(step + TRANSPOSE_LEAD)
+            for i in range(PAIR):
+                j = step * PAIR + i
+                if 0 <= j:
+                    activate(j)
+                    transpose_back(j)
+                if 0 <= j + Y_BANKS < TILES:
+                    multiply_and_gate(j + Y_BANKS)
+                if i == 0 and step + INPUT_LEAD < STEPS:
+                    transpose_half(step + INPUT_LEAD)
+                if 0 <= j - 1:
+                    add_residual(j - 1)
+                group, second = divmod(step + QUANTISE_LEAD, STEPS_PER_GROUP)
+                if i == 0 and second == 0 and 0 <= group < GROUPS:
+                    quantise(group)
+            if step + INPUT_LEAD < STEPS:
+                normalise_half(step + INPUT_LEAD)
 
-        for step in range(-TRANSPOSE_LEAD, XT_BANKS - TRANSPOSE_LEAD):
+        for step in range(-INPUT_LEAD, XT_BANKS - INPUT_LEAD):
             run_step(step)
         make_tables()
-        for step in range(XT_BANKS - TRANSPOSE_LEAD, STEPS):
+        for step in range(XT_BANKS - INPUT_LEAD, STEPS):
             run_step(step)
+        add_residual(TILES - 1)

@@ -44,7 +44,6 @@ def tile_better_transformer_t_e_kernel(
 ):
     nc = tc.nc
     with ExitStack() as ctx:
-        ctx.enter_context(tc.manual_schedule())
         const = ctx.enter_context(tc.tile_pool(name="const", bufs=1))
         x_pool = ctx.enter_context(tc.tile_pool(name="x_pool", bufs=ROUNDS))
         grouped_pool = ctx.enter_context(tc.tile_pool(name="grouped_pool", bufs=2))

@@ -33,8 +33,6 @@ HALF = ROUND // 2
 N_COLS = FEATURES // P
 XT_BANKS = 2
 Y_BANKS = 4
-INPUT_LEAD = 6
-QUANTISE_LEAD = 3
 
 FLOPS = 2 * ROWS * FEATURES * PART
 
@@ -256,27 +254,16 @@ def tile_better_transformer_t_e_kernel(
                     in_=out_tiles[step][:],
                 )
 
-        def run_step(step):
-            for i in range(PAIR):
-                j = step * PAIR + i
-                if 0 <= j:
-                    activate(j)
-                    transpose_back(j)
-                if 0 <= j + Y_BANKS < TILES:
-                    multiply_and_gate(j + Y_BANKS)
-                if i == 0 and step + INPUT_LEAD < STEPS:
-                    transpose_half(step + INPUT_LEAD)
-                if 0 <= j - 1:
-                    add_residual(j - 1)
-                group, second = divmod(step + QUANTISE_LEAD, STEPS_PER_GROUP)
-                if i == 0 and second == 0 and 0 <= group < GROUPS:
-                    quantise(group)
-            if step + INPUT_LEAD < STEPS:
-                normalise_half(step + INPUT_LEAD)
-
-        for step in range(-INPUT_LEAD, XT_BANKS - INPUT_LEAD):
-            run_step(step)
-        make_tables()
-        for step in range(XT_BANKS - INPUT_LEAD, STEPS):
-            run_step(step)
-        add_residual(TILES - 1)
+        for group in range(GROUPS):
+            for h in range(2):
+                transpose_half(2 * group + h)
+                normalise_half(2 * group + h)
+            if group == 0:
+                make_tables()
+            quantise(group)
+            for m in range(F_TILES):
+                j = group * F_TILES + m
+                multiply_and_gate(j)
+                activate(j)
+                transpose_back(j)
+                add_residual(j)

@@ -33,6 +33,8 @@ HALF = ROUND // 2
 N_COLS = FEATURES // P
 XT_BANKS = 2
 Y_BANKS = 4
+INPUT_LEAD = 6
+QUANTISE_LEAD = 3
 
 FLOPS = 2 * ROWS * FEATURES * PART
 
@@ -58,9 +60,11 @@ def tile_better_transformer_t_e_kernel(
 
         def load_round(r):
             x_sb = x_pool.tile([P, ROW_TILES, FEATURES], BF16)
-            for h in range(2):
-                tiles = slice(2 * h, 2 * h + 2)
-                nc.sync.dma_start(out=x_sb[:, tiles, :], in_=x_rounds[r, :, tiles, :])
+            for g in range(PARTS):
+                for h in range(2):
+                    tiles = slice(2 * h, 2 * h + 2)
+                    part = slice(g * PART, (g + 1) * PART)
+                    nc.sync.dma_start(out=x_sb[:, tiles, part], in_=x_rounds[r, :, tiles, part])
             return x_sb
 
         x_tiles = [load_round(0)]
@@ -160,15 +164,27 @@ def tile_better_transformer_t_e_kernel(
                 grouped = grouped_pool.tile([P, ROUND, PACK], BF16, align_bytes=64)
                 grouped_tiles[group] = grouped
             xt_ps = transposed[half]
-            nc.scalar.activation(
-                out=grouped_tiles[group][:, h * HALF : (h + 1) * HALF, :].rearrange(
-                    "p c (u e) -> p c u e", e=2
-                ),
-                in_=xt_ps[:].bitcast(BF16).rearrange("p u (c e) -> p c u e", e=2),
-                func=ACT.Identity,
-                scale=gain_col[:, 0:1],
-                bias=norm_bias_col[:, 0:1],
+            x_norm = grouped_tiles[group][:, h * HALF : (h + 1) * HALF, :].rearrange(
+                "p c (u e) -> p c u e", e=2
             )
+            x_t = xt_ps[:].bitcast(BF16).rearrange("p u (c e) -> p c u e", e=2)
+            if half < INPUT_LEAD and h == 1:
+                nc.vector.tensor_scalar(
+                    out=x_norm,
+                    in0=x_t,
+                    scalar1=gain_col[:, 0:1],
+                    scalar2=norm_bias_col[:, 0:1],
+                    op0=ALU.mult,
+                    op1=ALU.add,
+                )
+            else:
+                nc.scalar.activation(
+                    out=x_norm,
+                    in_=x_t,
+                    func=ACT.Identity,
+                    scale=gain_col[:, 0:1],
+                    bias=norm_bias_col[:, 0:1],
+                )
 
         def quantise(group):
             codes = codes_pool.tile([P, ROUND], U32, align_bytes=64)
@@ -254,16 +270,27 @@ def tile_better_transformer_t_e_kernel(
                     in_=out_tiles[step][:],
                 )
 
-        for group in range(GROUPS):
-            for h in range(2):
-                transpose_half(2 * group + h)
-                normalise_half(2 * group + h)
-            if group == 0:
-                make_tables()
-            quantise(group)
-            for m in range(F_TILES):
-                j = group * F_TILES + m
-                multiply_and_gate(j)
-                activate(j)
-                transpose_back(j)
-                add_residual(j)
+        def run_step(step):
+            for i in range(PAIR):
+                j = step * PAIR + i
+                if 0 <= j:
+                    activate(j)
+                    transpose_back(j)
+                if 0 <= j + Y_BANKS < TILES:
+                    multiply_and_gate(j + Y_BANKS)
+                if i == 0 and step + INPUT_LEAD < STEPS:
+                    transpose_half(step + INPUT_LEAD)
+                if 0 <= j - 1:
+                    add_residual(j - 1)
+                group, second = divmod(step + QUANTISE_LEAD, STEPS_PER_GROUP)
+                if i == 0 and second == 0 and 0 <= group < GROUPS:
+                    quantise(group)
+            if step + INPUT_LEAD < STEPS:
+                normalise_half(step + INPUT_LEAD)
+
+        for step in range(-INPUT_LEAD, XT_BANKS - INPUT_LEAD):
+            run_step(step)
+        make_tables()
+        for step in range(XT_BANKS - INPUT_LEAD, STEPS):
+            run_step(step)
+        add_residual(TILES - 1)

@@ -35,6 +35,7 @@ XT_BANKS = 2
 Y_BANKS = 4
 INPUT_LEAD = 6
 QUANTISE_LEAD = 3
+SCALAR_EVERY = 5
 
 FLOPS = 2 * ROWS * FEATURES * PART
 
@@ -102,6 +103,8 @@ def tile_better_transformer_t_e_kernel(
 
         ident = const.tile([P, P], F32)
         make_identity(nc, ident[:])
+        ident_bf = const.tile([P, P], BF16)
+        make_identity(nc, ident_bf[:])
 
         warm = const.tile([P, 1], F32)
         nc.vector.memset(warm[:], 0.0)
@@ -244,10 +247,36 @@ def tile_better_transformer_t_e_kernel(
             )
             acts[j] = act
 
+        def by_scalar(j):
+            return j % SCALAR_EVERY == SCALAR_EVERY - 1
+
         def transpose_back(j):
             back_ps = back_psum.tile([P, ROW_TILES, P], F32)
-            for t in range(ROW_TILES):
-                nc.tensor.transpose(back_ps[:, t, :], acts[j][:, t * P : (t + 1) * P], ident[:])
+            if by_scalar(j):
+                group, m = divmod(j, F_TILES)
+                r, g = divmod(group, PARTS)
+                first = g * PART + m * P
+                nc.tensor.matmul(
+                    out=back_ps[:],
+                    lhsT=ident_bf[:],
+                    rhs=x_tiles[r][:, :, first : first + P],
+                    start=True,
+                    stop=False,
+                )
+                for t in range(ROW_TILES):
+                    nc.tensor.matmul(
+                        out=back_ps[:, t, :],
+                        lhsT=acts[j][:, t * P : (t + 1) * P],
+                        rhs=ident[:],
+                        is_transpose=True,
+                        start=False,
+                        stop=(t == ROW_TILES - 1),
+                    )
+            else:
+                for t in range(ROW_TILES):
+                    nc.tensor.transpose(
+                        back_ps[:, t, :], acts[j][:, t * P : (t + 1) * P], ident[:]
+                    )
             backs[j] = back_ps
 
         def add_residual(j):
@@ -258,12 +287,15 @@ def tile_better_transformer_t_e_kernel(
                 out_sb = out_pool.tile([P, ROW_TILES, PAIR * P], F32)
                 out_tiles[step] = out_sb
             first = g * PART + m * P
-            nc.vector.tensor_tensor(
-                out=out_tiles[step][:, :, i * P : (i + 1) * P],
-                in0=backs[j][:],
-                in1=x_tiles[r][:, :, first : first + P],
-                op=ALU.add,
-            )
+            if by_scalar(j):
+                nc.scalar.copy(out=out_tiles[step][:, :, i * P : (i + 1) * P], in_=backs[j][:])
+            else:
+                nc.vector.tensor_tensor(
+                    out=out_tiles[step][:, :, i * P : (i + 1) * P],
+                    in0=backs[j][:],
+                    in1=x_tiles[r][:, :, first : first + P],
+                    op=ALU.add,
+                )
             if i == PAIR - 1:
                 nc.sync.dma_start(
                     out=out_rounds[r, :, :, first + P - PAIR * P : first + P],

@@ -250,8 +250,9 @@ def tile_better_transformer_t_e_kernel(
         def by_scalar(j):
             return j % SCALAR_EVERY == SCALAR_EVERY - 1
 
-        def transpose_back(j):
+        def open_back(j):
             back_ps = back_psum.tile([P, ROW_TILES, P], F32)
+            backs[j] = back_ps
             if by_scalar(j):
                 group, m = divmod(j, F_TILES)
                 r, g = divmod(group, PARTS)
@@ -263,6 +264,10 @@ def tile_better_transformer_t_e_kernel(
                     start=True,
                     stop=False,
                 )
+
+        def transpose_back(j):
+            back_ps = backs[j]
+            if by_scalar(j):
                 for t in range(ROW_TILES):
                     nc.tensor.matmul(
                         out=back_ps[:, t, :],
@@ -277,7 +282,6 @@ def tile_better_transformer_t_e_kernel(
                     nc.tensor.transpose(
                         back_ps[:, t, :], acts[j][:, t * P : (t + 1) * P], ident[:]
                     )
-            backs[j] = back_ps
 
         def add_residual(j):
             step, i = divmod(j, PAIR)
@@ -303,26 +307,34 @@ def tile_better_transformer_t_e_kernel(
                 )
 
         def run_step(step):
-            for i in range(PAIR):
-                j = step * PAIR + i
+            pair = (step * PAIR, step * PAIR + 1)
+            for j in pair:
                 if 0 <= j:
                     activate(j)
-                    transpose_back(j)
+            for j in pair:
                 if 0 <= j + Y_BANKS < TILES:
                     multiply_and_gate(j + Y_BANKS)
-                if i == 0 and step + INPUT_LEAD < STEPS:
-                    transpose_half(step + INPUT_LEAD)
-                if 0 <= j - 1:
-                    add_residual(j - 1)
-                group, second = divmod(step + QUANTISE_LEAD, STEPS_PER_GROUP)
-                if i == 0 and second == 0 and 0 <= group < GROUPS:
-                    quantise(group)
+            group, second = divmod(step + QUANTISE_LEAD, STEPS_PER_GROUP)
+            if second == 0 and 0 <= group < GROUPS:
+                quantise(group)
+            for j in pair:
+                if 0 <= j - PAIR:
+                    add_residual(j - PAIR)
+            for j in pair:
+                if 0 <= j:
+                    open_back(j)
+            for j in pair:
+                if 0 <= j:
+                    transpose_back(j)
             if step + INPUT_LEAD < STEPS:
+                transpose_half(step + INPUT_LEAD)
                 normalise_half(step + INPUT_LEAD)
 
-        for step in range(-INPUT_LEAD, XT_BANKS - INPUT_LEAD):
-            run_step(step)
-        make_tables()
-        for step in range(XT_BANKS - INPUT_LEAD, STEPS):
-            run_step(step)
-        add_residual(TILES - 1)
+        with tc.manual_schedule(engines={mybir.EngineType.PE}):
+            for step in range(-INPUT_LEAD, XT_BANKS - INPUT_LEAD):
+                run_step(step)
+            make_tables()
+            for step in range(XT_BANKS - INPUT_LEAD, STEPS):
+                run_step(step)
+            for j in (TILES - PAIR, TILES - 1):
+                add_residual(j)

@@ -31,8 +31,9 @@ STEPS = TILES // PAIR
 STEPS_PER_GROUP = F_TILES // PAIR
 HALF = ROUND // 2
 N_COLS = FEATURES // P
-XT_BANKS = 2
+XT_BANKS = 1
 Y_BANKS = 4
+BACK_BANKS = 3
 INPUT_LEAD = 6
 QUANTISE_LEAD = 3
 SCALAR_EVERY = 5
@@ -54,7 +55,7 @@ def tile_better_transformer_t_e_kernel(
         out_pool = ctx.enter_context(tc.tile_pool(name="out_pool", bufs=4))
         xt_psum = ctx.enter_context(tc.psum_pool(name="xt_psum", bufs=XT_BANKS))
         y_psum = ctx.enter_context(tc.psum_pool(name="y_psum", bufs=Y_BANKS))
-        back_psum = ctx.enter_context(tc.psum_pool(name="back_psum", bufs=PAIR))
+        back_psum = ctx.enter_context(tc.psum_pool(name="back_psum", bufs=BACK_BANKS))
 
         x_rounds = x.rearrange("(r p t) f -> r p t f", p=P, t=ROW_TILES)
         out_rounds = out.rearrange("(r p t) f -> r p t f", p=P, t=ROW_TILES)
@@ -151,7 +152,10 @@ def tile_better_transformer_t_e_kernel(
             r, g = divmod(group, PARTS)
             x_words = x_tiles[r][:].bitcast(F32)
             first_word = g * PART // 2
-            xt_ps = xt_psum.tile([P, 2, HALF], F32)
+            if half < INPUT_LEAD and half % 2 == 1:
+                xt_ps = back_psum.tile([P, 2, HALF], F32, name="back_ps")
+            else:
+                xt_ps = xt_psum.tile([P, 2, HALF], F32)
             for i in range(2):
                 for u in range(2):
                     nc.tensor.transpose(

@@ -37,6 +37,7 @@ BACK_BANKS = 3
 INPUT_LEAD = 6
 QUANTISE_LEAD = 3
 SCALAR_EVERY = 5
+VECTOR_EVERY = 4
 
 FLOPS = 2 * ROWS * FEATURES * PART
 
@@ -175,7 +176,7 @@ def tile_better_transformer_t_e_kernel(
                 "p c (u e) -> p c u e", e=2
             )
             x_t = xt_ps[:].bitcast(BF16).rearrange("p u (c e) -> p c u e", e=2)
-            if half < INPUT_LEAD and h == 1:
+            if (half < INPUT_LEAD and h == 1) or half % VECTOR_EVERY == 1:
                 nc.vector.tensor_scalar(
                     out=x_norm,
                     in0=x_t,
@@ -252,7 +253,7 @@ def tile_better_transformer_t_e_kernel(
             acts[j] = act
 
         def by_scalar(j):
-            return j % SCALAR_EVERY == SCALAR_EVERY - 1
+            return j % SCALAR_EVERY in (1, SCALAR_EVERY - 1)
 
         def open_back(j):
             back_ps = back_psum.tile([P, ROW_TILES, P], F32)

@@ -37,7 +37,7 @@ BACK_BANKS = 3
 INPUT_LEAD = 6
 QUANTISE_LEAD = 3
 SCALAR_EVERY = 5
-VECTOR_EVERY = 4
+VECTOR_EVERY = 2
 
 FLOPS = 2 * ROWS * FEATURES * PART
 

@@ -176,7 +176,7 @@ def tile_better_transformer_t_e_kernel(
                 "p c (u e) -> p c u e", e=2
             )
             x_t = xt_ps[:].bitcast(BF16).rearrange("p u (c e) -> p c u e", e=2)
-            if (half < INPUT_LEAD and h == 1) or half % VECTOR_EVERY == 1:
+            if on_vector(half):
                 nc.vector.tensor_scalar(
                     out=x_norm,
                     in0=x_t,
@@ -292,7 +292,7 @@ def tile_better_transformer_t_e_kernel(
             step, i = divmod(j, PAIR)
             group, m = divmod(j, F_TILES)
             r, g = divmod(group, PARTS)
-            if i == 0:
+            if step not in out_tiles:
                 out_sb = out_pool.tile([P, ROW_TILES, PAIR * P], F32)
                 out_tiles[step] = out_sb
             first = g * PART + m * P
@@ -305,16 +305,29 @@ def tile_better_transformer_t_e_kernel(
                     in1=x_tiles[r][:, :, first : first + P],
                     op=ALU.add,
                 )
-            if i == PAIR - 1:
-                nc.sync.dma_start(
-                    out=out_rounds[r, :, :, first + P - PAIR * P : first + P],
-                    in_=out_tiles[step][:],
-                )
+
+        def store_pair(step):
+            group, m = divmod(step * PAIR, F_TILES)
+            r, g = divmod(group, PARTS)
+            first = g * PART + m * P
+            nc.sync.dma_start(
+                out=out_rounds[r, :, :, first : first + PAIR * P], in_=out_tiles[step][:]
+            )
+
+        def on_vector(half):
+            return (half < INPUT_LEAD and half % 2 == 1) or half % VECTOR_EVERY == 1
 
         def run_step(step):
             pair = (step * PAIR, step * PAIR + 1)
+            before = [j - PAIR for j in pair if 0 <= j - PAIR < TILES]
+            late_half = step + INPUT_LEAD - 1
+            for j in before:
+                if by_scalar(j):
+                    add_residual(j)
+            if 0 <= late_half < STEPS and not on_vector(late_half):
+                normalise_half(late_half)
             for j in pair:
-                if 0 <= j:
+                if 0 <= j < TILES:
                     activate(j)
             for j in pair:
                 if 0 <= j + Y_BANKS < TILES:
@@ -322,24 +335,25 @@ def tile_better_transformer_t_e_kernel(
             group, second = divmod(step + QUANTISE_LEAD, STEPS_PER_GROUP)
             if second == 0 and 0 <= group < GROUPS:
                 quantise(group)
+            for j in before:
+                if not by_scalar(j):
+                    add_residual(j)
+            if 0 <= late_half < STEPS and on_vector(late_half):
+                normalise_half(late_half)
+            if before:
+                store_pair(step - 1)
             for j in pair:
-                if 0 <= j - PAIR:
-                    add_residual(j - PAIR)
-            for j in pair:
-                if 0 <= j:
+                if 0 <= j < TILES:
                     open_back(j)
             for j in pair:
-                if 0 <= j:
+                if 0 <= j < TILES:
                     transpose_back(j)
             if step + INPUT_LEAD < STEPS:
                 transpose_half(step + INPUT_LEAD)
-                normalise_half(step + INPUT_LEAD)
 
-        with tc.manual_schedule(engines={mybir.EngineType.PE}):
+        with tc.manual_schedule():
             for step in range(-INPUT_LEAD, XT_BANKS - INPUT_LEAD):
                 run_step(step)
             make_tables()
-            for step in range(XT_BANKS - INPUT_LEAD, STEPS):
+            for step in range(XT_BANKS - INPUT_LEAD, STEPS + 1):
                 run_step(step)
-            for j in (TILES - PAIR, TILES - 1):
-                add_residual(j)

@@ -48,7 +48,7 @@ def tile_better_transformer_t_e_kernel(
     nc = tc.nc
     with ExitStack() as ctx:
         const = ctx.enter_context(tc.tile_pool(name="const", bufs=1))
-        x_pool = ctx.enter_context(tc.tile_pool(name="x_pool", bufs=ROUNDS))
+        x_pool = ctx.enter_context(tc.tile_pool(name="x_pool", bufs=GROUPS))
         grouped_pool = ctx.enter_context(tc.tile_pool(name="grouped_pool", bufs=2))
         codes_pool = ctx.enter_context(tc.tile_pool(name="codes_pool", bufs=3))
         gate_pool = ctx.enter_context(tc.tile_pool(name="gate_pool", bufs=Y_BANKS + 2))
@@ -62,13 +62,15 @@ def tile_better_transformer_t_e_kernel(
         out_rounds = out.rearrange("(r p t) f -> r p t f", p=P, t=ROW_TILES)
 
         def load_round(r):
-            x_sb = x_pool.tile([P, ROW_TILES, FEATURES], BF16)
+            parts = []
             for g in range(PARTS):
+                x_sb = x_pool.tile([P, ROW_TILES, PART], BF16)
+                parts.append(x_sb)
                 for h in range(2):
                     tiles = slice(2 * h, 2 * h + 2)
                     part = slice(g * PART, (g + 1) * PART)
-                    nc.sync.dma_start(out=x_sb[:, tiles, part], in_=x_rounds[r, :, tiles, part])
-            return x_sb
+                    nc.sync.dma_start(out=x_sb[:, tiles, :], in_=x_rounds[r, :, tiles, part])
+            return parts
 
         x_tiles = [load_round(0)]
 
@@ -151,8 +153,7 @@ def tile_better_transformer_t_e_kernel(
         def transpose_half(half):
             group, h = divmod(half, 2)
             r, g = divmod(group, PARTS)
-            x_words = x_tiles[r][:].bitcast(F32)
-            first_word = g * PART // 2
+            x_words = x_tiles[r][g][:].bitcast(F32)
             if half < INPUT_LEAD and half % 2 == 1:
                 xt_ps = back_psum.tile([P, 2, HALF], F32, name="back_ps")
             else:
@@ -161,7 +162,7 @@ def tile_better_transformer_t_e_kernel(
                 for u in range(2):
                     nc.tensor.transpose(
                         xt_ps[:, u, i * P : (i + 1) * P],
-                        x_words[:, 2 * h + i, first_word + u : first_word + PART // 2 : 2],
+                        x_words[:, 2 * h + i, u : PART // 2 : 2],
                         ident[:],
                     )
             transposed[half] = xt_ps
@@ -261,11 +262,10 @@ def tile_better_transformer_t_e_kernel(
             if by_scalar(j):
                 group, m = divmod(j, F_TILES)
                 r, g = divmod(group, PARTS)
-                first = g * PART + m * P
                 nc.tensor.matmul(
                     out=back_ps[:],
                     lhsT=ident_bf[:],
-                    rhs=x_tiles[r][:, :, first : first + P],
+                    rhs=x_tiles[r][g][:, :, m * P : (m + 1) * P],
                     start=True,
                     stop=False,
                 )
@@ -295,14 +295,13 @@ def tile_better_transformer_t_e_kernel(
             if step not in out_tiles:
                 out_sb = out_pool.tile([P, ROW_TILES, PAIR * P], F32)
                 out_tiles[step] = out_sb
-            first = g * PART + m * P
             if by_scalar(j):
                 nc.scalar.copy(out=out_tiles[step][:, :, i * P : (i + 1) * P], in_=backs[j][:])
             else:
                 nc.vector.tensor_tensor(
                     out=out_tiles[step][:, :, i * P : (i + 1) * P],
                     in0=backs[j][:],
-                    in1=x_tiles[r][:, :, first : first + P],
+                    in1=x_tiles[r][g][:, :, m * P : (m + 1) * P],
                     op=ALU.add,
                 )
 

@@ -254,7 +254,7 @@ def tile_better_transformer_t_e_kernel(
             acts[j] = act
 
         def by_scalar(j):
-            return j % SCALAR_EVERY in (1, SCALAR_EVERY - 1)
+            return j % 5 in (2, 4)
 
         def open_back(j):
             back_ps = back_psum.tile([P, ROW_TILES, P], F32)
@@ -331,12 +331,12 @@ def tile_better_transformer_t_e_kernel(
             for j in pair:
                 if 0 <= j + Y_BANKS < TILES:
                     multiply_and_gate(j + Y_BANKS)
-            group, second = divmod(step + QUANTISE_LEAD, STEPS_PER_GROUP)
-            if second == 0 and 0 <= group < GROUPS:
-                quantise(group)
             for j in before:
                 if not by_scalar(j):
                     add_residual(j)
+            group, second = divmod(step + QUANTISE_LEAD, STEPS_PER_GROUP)
+            if second == 0 and 0 <= group < GROUPS:
+                quantise(group)
             if 0 <= late_half < STEPS and on_vector(late_half):
                 normalise_half(late_half)
             if before:

@@ -61,63 +61,63 @@ def tile_better_transformer_t_e_kernel(
         x_rounds = x.rearrange("(r p t) f -> r p t f", p=P, t=ROW_TILES)
         out_rounds = out.rearrange("(r p t) f -> r p t f", p=P, t=ROW_TILES)
 
-        def load_round(r):
-            parts = []
+        x_tiles = [[], []]
+        for r in range(ROUNDS):
             for g in range(PARTS):
                 x_sb = x_pool.tile([P, ROW_TILES, PART], BF16)
-                parts.append(x_sb)
-                for h in range(2):
-                    tiles = slice(2 * h, 2 * h + 2)
-                    part = slice(g * PART, (g + 1) * PART)
-                    nc.sync.dma_start(out=x_sb[:, tiles, :], in_=x_rounds[r, :, tiles, part])
-            return parts
+                x_tiles[g].append(x_sb)
 
-        x_tiles = [load_round(0)]
+        def load_half(half):
+            group, h = divmod(half, 2)
+            r, g = divmod(group, PARTS)
+            tiles = slice(2 * h, 2 * h + 2)
+            part = slice(g * PART, (g + 1) * PART)
+            nc.sync.dma_start(out=x_tiles[g][r][:, tiles, :], in_=x_rounds[r, :, tiles, part])
 
         gain_bf = const.tile([P, 1], BF16)
-        nc.scalar.dma_start(out=gain_bf[:], in_=gain.partition_broadcast(P))
         norm_bias_bf = const.tile([P, 1], BF16)
-        nc.scalar.dma_start(out=norm_bias_bf[:], in_=norm_bias.partition_broadcast(P))
-
-        w_words = const.tile([P, PARTS, 2 * PART], U8, align_bytes=64)
-        nc.sync.dma_start(
-            out=w_words[:].bitcast(I32),
-            in_=weights_words.rearrange("g p n -> p g n").bitcast(I32),
-        )
-        w_scales = const.tile([P, PARTS, PART], U8, align_bytes=64)
-        nc.vector.memset(w_scales[:].bitcast(I32), 0)
-        for quadrant in range(4):
-            nc.sync.dma_start(
-                out=w_scales[32 * quadrant : 32 * quadrant + 4].bitcast(I32),
-                in_=weights_scales[:, 4 * quadrant : 4 * quadrant + 4, :]
-                .rearrange("g q n -> q g n")
-                .bitcast(I32),
-            )
-
-        for r in range(1, ROUNDS):
-            x_tiles.append(load_round(r))
-
-        rows_bf = const.tile([P, P], BF16)
-        nc.vector.memset(rows_bf[:], 0.0)
-        for i, vector in enumerate((bias, beta, gamma)):
-            nc.scalar.dma_start(
-                out=rows_bf[i * N_COLS : (i + 1) * N_COLS, :],
-                in_=vector.rearrange("(j p) -> j p", p=P),
-            )
-
-        ident = const.tile([P, P], F32)
-        make_identity(nc, ident[:])
-        ident_bf = const.tile([P, P], BF16)
-        make_identity(nc, ident_bf[:])
-
-        warm = const.tile([P, 1], F32)
-        nc.vector.memset(warm[:], 0.0)
-        nc.scalar.activation(out=warm[:], in_=warm[:], func=ACT.Sigmoid)
-
         gain_col = const.tile([P, 1], F32)
-        nc.vector.tensor_copy(out=gain_col[:], in_=gain_bf[:])
         norm_bias_col = const.tile([P, 1], F32)
-        nc.vector.tensor_copy(out=norm_bias_col[:], in_=norm_bias_bf[:])
+        w_words = const.tile([P, PARTS, 2 * PART], U8, align_bytes=64)
+        w_scales = const.tile([P, PARTS, PART], U8, align_bytes=64)
+        rows_bf = const.tile([P, P], BF16)
+        ident = const.tile([P, P], F32)
+        ident_bf = const.tile([P, P], BF16)
+        warm = const.tile([P, 1], F32)
+
+        def load():
+            nc.vector.memset(rows_bf[:], 0.0)
+            nc.vector.memset(w_scales[:].bitcast(I32), 0)
+            nc.vector.memset(warm[:], 0.0)
+            nc.scalar.activation(out=warm[:], in_=warm[:], func=ACT.Sigmoid)
+            make_identity(nc, ident[:])
+            make_identity(nc, ident_bf[:])
+            nc.sync.dma_start(out=gain_bf[:], in_=gain.partition_broadcast(P))
+            nc.sync.dma_start(out=norm_bias_bf[:], in_=norm_bias.partition_broadcast(P))
+            load_half(0)
+            load_half(1)
+            for i, vector in enumerate((bias, beta, gamma)):
+                nc.sync.dma_start(
+                    out=rows_bf[i * N_COLS : (i + 1) * N_COLS, :],
+                    in_=vector.rearrange("(j p) -> j p", p=P),
+                )
+            load_half(2)
+            load_half(3)
+            nc.sync.dma_start(
+                out=w_words[:].bitcast(I32),
+                in_=weights_words.rearrange("g p n -> p g n").bitcast(I32),
+            )
+            for quadrant in range(4):
+                nc.sync.dma_start(
+                    out=w_scales[32 * quadrant : 32 * quadrant + 4].bitcast(I32),
+                    in_=weights_scales[:, 4 * quadrant : 4 * quadrant + 4, :]
+                    .rearrange("g q n -> q g n")
+                    .bitcast(I32),
+                )
+            for half in range(4, 2 * GROUPS):
+                load_half(half)
+            nc.vector.tensor_copy(out=gain_col[:], in_=gain_bf[:])
+            nc.vector.tensor_copy(out=norm_bias_col[:], in_=norm_bias_bf[:])
 
         cols = const.tile([P, 3 * N_COLS], F32)
         bias_cols = cols[:, 0:N_COLS]
@@ -153,7 +153,7 @@ def tile_better_transformer_t_e_kernel(
         def transpose_half(half):
             group, h = divmod(half, 2)
             r, g = divmod(group, PARTS)
-            x_words = x_tiles[r][g][:].bitcast(F32)
+            x_words = x_tiles[g][r][:].bitcast(F32)
             if half < INPUT_LEAD and half % 2 == 1:
                 xt_ps = back_psum.tile([P, 2, HALF], F32, name="back_ps")
             else:
@@ -265,7 +265,7 @@ def tile_better_transformer_t_e_kernel(
                 nc.tensor.matmul(
                     out=back_ps[:],
                     lhsT=ident_bf[:],
-                    rhs=x_tiles[r][g][:, :, m * P : (m + 1) * P],
+                    rhs=x_tiles[g][r][:, :, m * P : (m + 1) * P],
                     start=True,
                     stop=False,
                 )
@@ -301,7 +301,7 @@ def tile_better_transformer_t_e_kernel(
                 nc.vector.tensor_tensor(
                     out=out_tiles[step][:, :, i * P : (i + 1) * P],
                     in0=backs[j][:],
-                    in1=x_tiles[r][g][:, :, m * P : (m + 1) * P],
+                    in1=x_tiles[g][r][:, :, m * P : (m + 1) * P],
                     op=ALU.add,
                 )
 
@@ -351,6 +351,7 @@ def tile_better_transformer_t_e_kernel(
                 transpose_half(step + INPUT_LEAD)
 
         with tc.manual_schedule():
+            load()
             for step in range(-INPUT_LEAD, XT_BANKS - INPUT_LEAD):
                 run_step(step)
             make_tables()

@@ -326,6 +326,9 @@ def tile_better_transformer_t_e_kernel(
             if 0 <= late_half < STEPS and not on_vector(late_half):
                 normalise_half(late_half)
             for j in pair:
+                if 0 <= j < TILES and by_scalar(j):
+                    open_back(j)
+            for j in pair:
                 if 0 <= j < TILES:
                     activate(j)
             for j in pair:
@@ -342,7 +345,7 @@ def tile_better_transformer_t_e_kernel(
             if before:
                 store_pair(step - 1)
             for j in pair:
-                if 0 <= j < TILES:
+                if 0 <= j < TILES and not by_scalar(j):
                     open_back(j)
             for j in pair:
                 if 0 <= j < TILES:

@@ -254,7 +254,7 @@ def tile_better_transformer_t_e_kernel(
             acts[j] = act
 
         def by_scalar(j):
-            return j % 5 in (2, 4)
+            return j % 2 == 0 and j % 10 != 2
 
         def open_back(j):
             back_ps = back_psum.tile([P, ROW_TILES, P], F32)

from contextlib import ExitStack

import concourse.mybir as mybir
from concourse.masks import make_identity

F32 = mybir.dt.float32
BF16 = mybir.dt.bfloat16
I32 = mybir.dt.int32
U32 = mybir.dt.uint32
U8 = mybir.dt.uint8
FP8X4 = mybir.dt.float8_e4m3fn_x4
FP4X4 = mybir.dt.float4_e2m1fn_x4
ALU = mybir.AluOpType
ACT = mybir.ActivationFunctionType

P = 128
PACK = 4
ROWS = 4096
PARTS = 2
PART = 512
FEATURES = PARTS * PART

ROUND = 512
ROW_TILES = ROUND // P
ROUNDS = ROWS // ROUND
GROUPS = ROUNDS * PARTS
F_TILES = PART // P
PAIR = 2
TILES = GROUPS * F_TILES
STEPS = TILES // PAIR
STEPS_PER_GROUP = F_TILES // PAIR
HALF = ROUND // 2
N_COLS = FEATURES // P
XT_BANKS = 1
Y_BANKS = 4
BACK_BANKS = 3
INPUT_LEAD = 6
QUANTISE_LEAD = 3
SCALAR_EVERY = 5
VECTOR_EVERY = 2

FLOPS = 2 * ROWS * FEATURES * PART


def tile_better_transformer_t_e_kernel(
    tc, x, weights_words, weights_scales, bias, gain, norm_bias, gamma, beta, out
):
    nc = tc.nc
    with ExitStack() as ctx:
        const = ctx.enter_context(tc.tile_pool(name="const", bufs=1))
        x_pool = ctx.enter_context(tc.tile_pool(name="x_pool", bufs=GROUPS))
        grouped_pool = ctx.enter_context(tc.tile_pool(name="grouped_pool", bufs=2))
        codes_pool = ctx.enter_context(tc.tile_pool(name="codes_pool", bufs=3))
        gate_pool = ctx.enter_context(tc.tile_pool(name="gate_pool", bufs=Y_BANKS + 2))
        act_pool = ctx.enter_context(tc.tile_pool(name="act_pool", bufs=2 * PAIR))
        out_pool = ctx.enter_context(tc.tile_pool(name="out_pool", bufs=4))
        xt_psum = ctx.enter_context(tc.psum_pool(name="xt_psum", bufs=XT_BANKS))
        y_psum = ctx.enter_context(tc.psum_pool(name="y_psum", bufs=Y_BANKS))
        back_psum = ctx.enter_context(tc.psum_pool(name="back_psum", bufs=BACK_BANKS))

        x_rounds = x.rearrange("(r p t) f -> r p t f", p=P, t=ROW_TILES)
        out_rounds = out.rearrange("(r p t) f -> r p t f", p=P, t=ROW_TILES)

        x_tiles = [[], []]
        for r in range(ROUNDS):
            for g in range(PARTS):
                x_sb = x_pool.tile([P, ROW_TILES, PART], BF16)
                x_tiles[g].append(x_sb)

        def load_half(half):
            group, h = divmod(half, 2)
            r, g = divmod(group, PARTS)
            tiles = slice(2 * h, 2 * h + 2)
            part = slice(g * PART, (g + 1) * PART)
            nc.sync.dma_start(out=x_tiles[g][r][:, tiles, :], in_=x_rounds[r, :, tiles, part])

        gain_bf = const.tile([P, 1], BF16)
        norm_bias_bf = const.tile([P, 1], BF16)
        gain_col = const.tile([P, 1], F32)
        norm_bias_col = const.tile([P, 1], F32)
        w_words = const.tile([P, PARTS, 2 * PART], U8, align_bytes=64)
        w_scales = const.tile([P, PARTS, PART], U8, align_bytes=64)
        rows_bf = const.tile([P, P], BF16)
        ident = const.tile([P, P], F32)
        ident_bf = const.tile([P, P], BF16)
        warm = const.tile([P, 1], F32)

        def load():
            nc.vector.memset(rows_bf[:], 0.0)
            nc.vector.memset(w_scales[:].bitcast(I32), 0)
            nc.vector.memset(warm[:], 0.0)
            nc.scalar.activation(out=warm[:], in_=warm[:], func=ACT.Sigmoid)
            make_identity(nc, ident[:])
            make_identity(nc, ident_bf[:])
            nc.sync.dma_start(out=gain_bf[:], in_=gain.partition_broadcast(P))
            nc.sync.dma_start(out=norm_bias_bf[:], in_=norm_bias.partition_broadcast(P))
            load_half(0)
            load_half(1)
            for i, vector in enumerate((bias, beta, gamma)):
                nc.sync.dma_start(
                    out=rows_bf[i * N_COLS : (i + 1) * N_COLS, :],
                    in_=vector.rearrange("(j p) -> j p", p=P),
                )
            load_half(2)
            load_half(3)
            nc.sync.dma_start(
                out=w_words[:].bitcast(I32),
                in_=weights_words.rearrange("g p n -> p g n").bitcast(I32),
            )
            for quadrant in range(4):
                nc.sync.dma_start(
                    out=w_scales[32 * quadrant : 32 * quadrant + 4].bitcast(I32),
                    in_=weights_scales[:, 4 * quadrant : 4 * quadrant + 4, :]
                    .rearrange("g q n -> q g n")
                    .bitcast(I32),
                )
            for half in range(4, 2 * GROUPS):
                load_half(half)
            nc.vector.tensor_copy(out=gain_col[:], in_=gain_bf[:])
            nc.vector.tensor_copy(out=norm_bias_col[:], in_=norm_bias_bf[:])

        cols = const.tile([P, 3 * N_COLS], F32)
        bias_cols = cols[:, 0:N_COLS]
        beta_cols = cols[:, N_COLS : 2 * N_COLS]
        gamma_cols = cols[:, 2 * N_COLS : 3 * N_COLS]
        beta_bias_cols = const.tile([P, N_COLS], F32)
        one_minus_gamma_cols = const.tile([P, N_COLS], F32)

        def make_tables():
            rows_f32 = const.tile([P, P], F32)
            nc.vector.tensor_copy(out=rows_f32[:], in_=rows_bf[:])
            cols_ps = back_psum.tile([P, ROW_TILES, P], F32, name="back_ps")
            nc.tensor.transpose(cols_ps[:, 0, :], rows_f32[:], ident[:])
            nc.vector.tensor_copy(out=cols[:], in_=cols_ps[:, 0, 0 : 3 * N_COLS])
            nc.vector.tensor_mul(out=beta_bias_cols[:], in0=beta_cols, in1=bias_cols)
            nc.vector.tensor_scalar(
                out=one_minus_gamma_cols[:],
                in0=gamma_cols,
                scalar1=-1.0,
                scalar2=1.0,
                op0=ALU.mult,
                op1=ALU.add,
            )

        transposed = {}
        grouped_tiles = {}
        operands = {}
        products = {}
        acts = {}
        backs = {}
        out_tiles = {}

        def transpose_half(half):
            group, h = divmod(half, 2)
            r, g = divmod(group, PARTS)
            x_words = x_tiles[g][r][:].bitcast(F32)
            if half < INPUT_LEAD and half % 2 == 1:
                xt_ps = back_psum.tile([P, 2, HALF], F32, name="back_ps")
            else:
                xt_ps = xt_psum.tile([P, 2, HALF], F32)
            for i in range(2):
                for u in range(2):
                    nc.tensor.transpose(
                        xt_ps[:, u, i * P : (i + 1) * P],
                        x_words[:, 2 * h + i, u : PART // 2 : 2],
                        ident[:],
                    )
            transposed[half] = xt_ps

        def normalise_half(half):
            group, h = divmod(half, 2)
            if h == 0:
                grouped = grouped_pool.tile([P, ROUND, PACK], BF16, align_bytes=64)
                grouped_tiles[group] = grouped
            xt_ps = transposed[half]
            x_norm = grouped_tiles[group][:, h * HALF : (h + 1) * HALF, :].rearrange(
                "p c (u e) -> p c u e", e=2
            )
            x_t = xt_ps[:].bitcast(BF16).rearrange("p u (c e) -> p c u e", e=2)
            if on_vector(half):
                nc.vector.tensor_scalar(
                    out=x_norm,
                    in0=x_t,
                    scalar1=gain_col[:, 0:1],
                    scalar2=norm_bias_col[:, 0:1],
                    op0=ALU.mult,
                    op1=ALU.add,
                )
            else:
                nc.scalar.activation(
                    out=x_norm,
                    in_=x_t,
                    func=ACT.Identity,
                    scale=gain_col[:, 0:1],
                    bias=norm_bias_col[:, 0:1],
                )

        def quantise(group):
            codes = codes_pool.tile([P, ROUND], U32, align_bytes=64)
            scales = codes_pool.tile([P, ROUND], U8, align_bytes=64)
            nc.vector.quantize_mx(
                out=codes[:].bitcast(FP8X4),
                scales=scales[:],
                in_=grouped_tiles[group][:].rearrange("p c j -> p (c j)"),
            )
            operands[group] = (codes, scales)

        def multiply_and_gate(j):
            group, m = divmod(j, F_TILES)
            g = group % PARTS
            col = g * F_TILES + m
            codes, scales = operands[group]
            y_ps = y_psum.tile([P, ROUND], F32)
            nc.tensor.matmul_mx(
                out=y_ps[:],
                lhsT=w_words[:, g, 2 * m * P : 2 * (m + 1) * P].bitcast(FP4X4),
                lhsT_scale=w_scales[:, g, m * P : (m + 1) * P],
                rhs=codes[:].bitcast(FP8X4),
                rhs_scale=scales[:],
                start=True,
                stop=True,
            )
            gate = gate_pool.tile([P, ROUND], F32)
            nc.scalar.activation(
                out=gate[:],
                in_=y_ps[:],
                func=ACT.Sigmoid,
                scale=beta_cols[:, col : col + 1],
                bias=beta_bias_cols[:, col : col + 1],
            )
            nc.gpsimd.tensor_scalar(
                out=gate[:],
                in0=gate[:],
                scalar1=one_minus_gamma_cols[:, col : col + 1],
                scalar2=gamma_cols[:, col : col + 1],
                op0=ALU.mult,
                op1=ALU.add,
            )
            products[j] = (y_ps, gate)

        def activate(j):
            group, m = divmod(j, F_TILES)
            col = (group % PARTS) * F_TILES + m
            y_ps, gate = products[j]
            act = act_pool.tile([P, ROUND], F32)
            nc.vector.scalar_tensor_tensor(
                out=act[:],
                in0=y_ps[:],
                scalar=bias_cols[:, col : col + 1],
                in1=gate[:],
                op0=ALU.add,
                op1=ALU.mult,
            )
            acts[j] = act

        def by_scalar(j):
            return j % 2 == 0 and j % 10 != 2

        def open_back(j):
            back_ps = back_psum.tile([P, ROW_TILES, P], F32)
            backs[j] = back_ps
            if by_scalar(j):
                group, m = divmod(j, F_TILES)
                r, g = divmod(group, PARTS)
                nc.tensor.matmul(
                    out=back_ps[:],
                    lhsT=ident_bf[:],
                    rhs=x_tiles[g][r][:, :, m * P : (m + 1) * P],
                    start=True,
                    stop=False,
                )

        def transpose_back(j):
            back_ps = backs[j]
            if by_scalar(j):
                for t in range(ROW_TILES):
                    nc.tensor.matmul(
                        out=back_ps[:, t, :],
                        lhsT=acts[j][:, t * P : (t + 1) * P],
                        rhs=ident[:],
                        is_transpose=True,
                        start=False,
                        stop=(t == ROW_TILES - 1),
                    )
            else:
                for t in range(ROW_TILES):
                    nc.tensor.transpose(
                        back_ps[:, t, :], acts[j][:, t * P : (t + 1) * P], ident[:]
                    )

        def add_residual(j):
            step, i = divmod(j, PAIR)
            group, m = divmod(j, F_TILES)
            r, g = divmod(group, PARTS)
            if step not in out_tiles:
                out_sb = out_pool.tile([P, ROW_TILES, PAIR * P], F32)
                out_tiles[step] = out_sb
            if by_scalar(j):
                nc.scalar.copy(out=out_tiles[step][:, :, i * P : (i + 1) * P], in_=backs[j][:])
            else:
                nc.vector.tensor_tensor(
                    out=out_tiles[step][:, :, i * P : (i + 1) * P],
                    in0=backs[j][:],
                    in1=x_tiles[g][r][:, :, m * P : (m + 1) * P],
                    op=ALU.add,
                )

        def store_pair(step):
            group, m = divmod(step * PAIR, F_TILES)
            r, g = divmod(group, PARTS)
            first = g * PART + m * P
            nc.sync.dma_start(
                out=out_rounds[r, :, :, first : first + PAIR * P], in_=out_tiles[step][:]
            )

        def on_vector(half):
            return (half < INPUT_LEAD and half % 2 == 1) or half % VECTOR_EVERY == 1

        def run_step(step):
            pair = (step * PAIR, step * PAIR + 1)
            before = [j - PAIR for j in pair if 0 <= j - PAIR < TILES]
            late_half = step + INPUT_LEAD - 1
            for j in before:
                if by_scalar(j):
                    add_residual(j)
            if 0 <= late_half < STEPS and not on_vector(late_half):
                normalise_half(late_half)
            for j in pair:
                if 0 <= j < TILES and by_scalar(j):
                    open_back(j)
            for j in pair:
                if 0 <= j < TILES:
                    activate(j)
            for j in pair:
                if 0 <= j + Y_BANKS < TILES:
                    multiply_and_gate(j + Y_BANKS)
            for j in before:
                if not by_scalar(j):
                    add_residual(j)
            group, second = divmod(step + QUANTISE_LEAD, STEPS_PER_GROUP)
            if second == 0 and 0 <= group < GROUPS:
                quantise(group)
            if 0 <= late_half < STEPS and on_vector(late_half):
                normalise_half(late_half)
            if before:
                store_pair(step - 1)
            for j in pair:
                if 0 <= j < TILES and not by_scalar(j):
                    open_back(j)
            for j in pair:
                if 0 <= j < TILES:
                    transpose_back(j)
            if step + INPUT_LEAD < STEPS:
                transpose_half(step + INPUT_LEAD)

        with tc.manual_schedule():
            load()
            for step in range(-INPUT_LEAD, XT_BANKS - INPUT_LEAD):
                run_step(step)
            make_tables()
            for step in range(XT_BANKS - INPUT_LEAD, STEPS + 1):
                run_step(step)
